import numpy as np
import ml_dtypes


def mxq(x, axis, fmt="e4m3"):
    dtype, down = {"e4m3": (ml_dtypes.float8_e4m3fn, 7), "e5m2": (ml_dtypes.float8_e5m2, 14)}[fmt]
    v = np.moveaxis(np.asarray(x, np.float32).astype(ml_dtypes.bfloat16).astype(np.float64), axis, -1)
    blocks = v.reshape(v.shape[:-1] + (-1, 32))
    amax = np.abs(blocks).max(-1, keepdims=True)
    byte = np.maximum(np.where(amax > 0, np.frexp(amax)[1] - 1 + 127, 0) - down, 1)
    scale = np.exp2(byte - 127.0)
    codes = (blocks / scale).astype(np.float32).astype(dtype).astype(np.float64)
    return np.moveaxis((codes * scale).reshape(v.shape), -1, axis)


WIDE = False


def mx_kscale(k):
    if not WIDE:
        return np.ones(k)
    levels = np.array([10, -10, 5, -5, 0])
    if k % 512:
        return np.exp2(np.random.permutation(np.resize(levels, k // 32))).repeat(32)
    a = np.empty((k // 512, 16))
    for p in range(k // 512):
        a[p, :8] = np.random.permutation(np.resize(levels, 8))
        for g in range(8):
            far = levels[np.abs(levels - a[p, g]) >= 10]
            a[p, g + 8] = far[np.random.randint(len(far))]
    return np.exp2(a.ravel()).repeat(32)


BF16 = ml_dtypes.bfloat16


def bf(x):
    return np.asarray(x, np.float32).astype(BF16)


def f64(x):
    return np.asarray(x).astype(np.float64)


N, K, F, H, O, Q, GS, SO = 1024, 8, 1024, 512, 256, 1024, 3, 2


def setup_inputs():
    s, t = mx_kscale(F), mx_kscale(H)
    return {"x": bf(np.random.standard_normal((N, F)) * s),
            "contexts": bf(np.random.standard_normal((N, K, F)) * s),
            "attn": bf(np.random.random((N, K))),
            "Wn": bf(np.random.standard_normal((H, F)) * 0.5 / np.sqrt(F) / s * t[:, None]),
            "bn": bf(np.random.standard_normal(H) * 0.1 * t),
            "Wc": bf(np.random.standard_normal((H, F)) * 1.5 / np.sqrt(F) / s * t[:, None]),
            "bc": bf(np.random.standard_normal(H) * 0.1 * t),
            "Wu": bf(np.random.standard_normal((O, H)) * 1.5 / np.sqrt(H) / t),
            "bu": bf(np.random.standard_normal(O) * 0.1)}


def reference(x, contexts, attn, Wn, bn, Wc, bc, Wu, bu):
    xt = (mxq(f64(x), 1, "e4m3") @ mxq(f64(Wn).T, 0, "e4m3")) + f64(bn)
    ct = (mxq(f64(contexts).reshape(N * K, F), 1, "e4m3") @ mxq(f64(Wc).T, 0, "e4m3")).reshape(N, K, H) + f64(bc)
    ca = (ct * f64(attn)[..., None]).mean(axis=1)
    return (mxq(xt + ca, 1, "e4m3") @ mxq(f64(Wu).T, 0, "e4m3")) + f64(bu)

@@ -1,0 +1,267 @@
+from contextlib import ExitStack
+
+import concourse.mybir as mybir
+from concourse.masks import make_identity
+
+F32 = mybir.dt.float32
+BF16 = mybir.dt.bfloat16
+U32 = mybir.dt.uint32
+U8 = mybir.dt.uint8
+FP8X4 = mybir.dt.float8_e4m3fn_x4
+ALU = mybir.AluOpType
+
+P = 128
+PACK = 4
+K_PASS = P * PACK
+
+NODES, CONTEXTS, FEATURES, HIDDEN, OUTPUTS = 1024, 8, 1024, 512, 256
+NODE_TILES = NODES // P
+PASSES = FEATURES // K_PASS
+WORD_PIECES = FEATURES // 2 // P
+
+BLOCKS = 4
+WN_ROUND = 0
+X_ROUND = 1
+WC_ROUND = X_ROUND + NODE_TILES // BLOCKS
+CONTEXT_ROUND = WC_ROUND + 1
+ROUNDS = CONTEXT_ROUND + NODE_TILES * CONTEXTS // BLOCKS
+ONE = CONTEXTS
+
+RAW_BUFS = 10 * BLOCKS
+BLOCK_BUFS = 3 * BLOCKS
+
+FLOPS = 2 * NODES * (CONTEXTS + 1) * FEATURES * HIDDEN + 2 * NODES * HIDDEN * OUTPUTS
+
+
+def tile_nodeembeddinglayer_pa_t_kernel(tc, x, contexts, attn, Wn, bn, Wc, bc, Wu, bu, out):
+    nc = tc.nc
+    with ExitStack() as stack:
+        keep = stack.enter_context(tc.tile_pool(name="keep", bufs=1))
+        raw_pool = stack.enter_context(tc.tile_pool(name="raw_pool", bufs=RAW_BUFS))
+        block_pool = stack.enter_context(tc.tile_pool(name="block_pool", bufs=BLOCK_BUFS))
+        tail_pool = stack.enter_context(tc.tile_pool(name="tail_pool", bufs=2))
+        flip_banks = stack.enter_context(tc.psum_pool(name="flip_banks", bufs=BLOCKS))
+        sum_banks = stack.enter_context(tc.psum_pool(name="sum_banks", bufs=BLOCKS))
+        stack.enter_context(tc.manual_schedule())
+
+        attn_sb = keep.tile([P, NODE_TILES, CONTEXTS], BF16)
+        nc.sync.dma_start(out=attn_sb[:], in_=attn.rearrange("(p t) k -> p t k", t=NODE_TILES))
+        BC, BN, BU = slice(0, HIDDEN), slice(HIDDEN, 2 * HIDDEN), slice(2 * HIDDEN, 2 * HIDDEN + OUTPUTS)
+        bias_rows = keep.tile([P, 2 * HIDDEN + OUTPUTS], BF16)
+        nc.vector.memset(bias_rows[:], 0.0)
+        nc.sync.dma_start(out=bias_rows[0:1, BC], in_=bc.unsqueeze(0))
+        nc.sync.dma_start(out=bias_rows[0:1, BN], in_=bn.unsqueeze(0))
+        nc.sync.dma_start(out=bias_rows[0:1, BU], in_=bu.unsqueeze(0))
+
+        x_blocks = x.rearrange("(p t) f -> t p f", t=NODE_TILES)
+        context_blocks = contexts.rearrange("(p t) k f -> (t k) p f", t=NODE_TILES)
+        wn_blocks = Wn.rearrange("(b p) f -> b p f", p=P)
+        wc_blocks = Wc.rearrange("(b p) f -> b p f", p=P)
+        sources = (
+            [wn_blocks[b] for b in range(BLOCKS)]
+            + [x_blocks[t] for t in range(NODE_TILES)]
+            + [wc_blocks[b] for b in range(BLOCKS)]
+            + [context_blocks[c] for c in range(NODE_TILES * CONTEXTS)]
+        )
+        out_tiles = out.rearrange("(p t) o -> t p o", t=NODE_TILES)
+
+        rows_of = {}
+
+        def load_block(i):
+            raw = raw_pool.tile([P, FEATURES], BF16)
+            nc.sync.dma_start(out=raw[:], in_=sources[i])
+            rows_of[i] = raw
+
+        for i in range(CONTEXT_ROUND * BLOCKS):
+            load_block(i)
+        wu_raw = keep.tile([P, OUTPUTS // P, HIDDEN], BF16)
+        nc.sync.dma_start(out=wu_raw[:], in_=Wu.rearrange("(b p) h -> p b h", p=P))
+        for i in range(CONTEXT_ROUND * BLOCKS, RAW_BUFS):
+            load_block(i)
+
+        identity_f32 = keep.tile([P, P], F32)
+        make_identity(nc, identity_f32[:])
+        identity_bf16 = keep.tile([P, P], BF16)
+        make_identity(nc, identity_bf16[:])
+        ones = keep.tile([P, P], BF16)
+        nc.vector.memset(ones[:], 1.0)
+
+        bias_all = keep.tile([P, 2 * HIDDEN + OUTPUTS], F32)
+        for cols, width in ((BC, HIDDEN), (BN, HIDDEN), (BU, OUTPUTS)):
+            spread = sum_banks.tile([P, width], F32, tag="sums")
+            nc.tensor.matmul(out=spread[:], lhsT=ones[:], rhs=bias_rows[:, cols], start=True, stop=True)
+            nc.scalar.copy(out=bias_all[:, cols], in_=spread[:])
+
+        weight = keep.tile([P, NODE_TILES, CONTEXTS + 1], F32)
+        nc.vector.memset(weight[:], 1.0)
+        nc.vector.tensor_scalar_mul(out=weight[:, :, 0:CONTEXTS], in0=attn_sb[:], scalar1=1.0 / CONTEXTS)
+        weight_sum = keep.tile([P, NODE_TILES], F32)
+        nc.vector.tensor_reduce(
+            out=weight_sum[:], in_=weight[:, :, 0:CONTEXTS], axis=mybir.AxisListType.X, op=ALU.add
+        )
+        running = keep.tile([P, NODE_TILES, HIDDEN], F32)
+        for t in range(NODE_TILES):
+            nc.vector.scalar_tensor_tensor(
+                out=running[:, t, :],
+                in0=bias_all[:, BC],
+                scalar=weight_sum[:, t : t + 1],
+                in1=bias_all[:, BN],
+                op0=ALU.mult,
+                op1=ALU.add,
+            )
+
+        def flip_block(i, grouped_words):
+            words = rows_of[i][:].bitcast(F32)
+            flipped = flip_banks.tile([P, WORD_PIECES, P], F32, tag="flipped")
+            for g in range(PASSES):
+                for u in range(2):
+                    piece = words[:, 2 * P * g + u : 2 * P * (g + 1) : 2]
+                    nc.tensor.transpose(flipped[:, 2 * g + u, :], piece, identity_f32[:])
+            nc.scalar.copy(out=grouped_words, in_=flipped[:].rearrange("p (g u) r -> p g r u", u=2))
+            if i + RAW_BUFS < len(sources):
+                load_block(i + RAW_BUFS)
+
+        def flip_round(q):
+            grouped_blocks = []
+            for j in range(BLOCKS):
+                grouped = block_pool.tile([P, PASSES * P * PACK], BF16, align_bytes=64)
+                flip_block(
+                    q * BLOCKS + j,
+                    grouped[:].bitcast(F32).rearrange("p (g r u) -> p g r u", g=PASSES, u=2),
+                )
+                grouped_blocks.append(grouped)
+            return grouped_blocks
+
+        def quantise_block(grouped):
+            codes = block_pool.tile([P, PASSES * P], U32, align_bytes=64)
+            scales = block_pool.tile([P, PASSES * P], U8, align_bytes=64)
+            nc.vector.quantize_mx(out=codes[:].bitcast(FP8X4), scales=scales[:], in_=grouped[:])
+            return codes, scales
+
+        def flip_weights(q, label):
+            grouped = keep.tile([P, PASSES * HIDDEN * PACK], BF16, align_bytes=64, name=label + "_grouped")
+            by_block = grouped[:].bitcast(F32).rearrange("p (g b r u) -> p b g r u", g=PASSES, b=BLOCKS, u=2)
+            for b in range(BLOCKS):
+                flip_block(q * BLOCKS + b, by_block[:, b])
+            return grouped
+
+        def quantise_weights(grouped, label):
+            codes = keep.tile([P, PASSES * HIDDEN], U32, align_bytes=64, name=label + "_codes")
+            scales = keep.tile([P, PASSES * HIDDEN], U8, align_bytes=64, name=label + "_scales")
+            nc.vector.quantize_mx(out=codes[:].bitcast(FP8X4), scales=scales[:], in_=grouped[:])
+            return codes, scales
+
+        def multiply_block(operand, weights):
+            codes, scales = operand
+            w_codes, w_scales = weights
+            sums = sum_banks.tile([P, HIDDEN], F32, tag="sums")
+            for g in range(PASSES):
+                rows = slice(g * P, (g + 1) * P)
+                hidden_cols = slice(g * HIDDEN, (g + 1) * HIDDEN)
+                nc.tensor.matmul_mx(
+                    out=sums[:],
+                    lhsT=codes[:, rows].bitcast(FP8X4),
+                    lhsT_scale=scales[:, rows],
+                    rhs=w_codes[:, hidden_cols].bitcast(FP8X4),
+                    rhs_scale=w_scales[:, hidden_cols],
+                    start=(g == 0),
+                    stop=(g == PASSES - 1),
+                )
+            return sums
+
+        def add_weighted(sums, t, column, target):
+            nc.vector.scalar_tensor_tensor(
+                out=target,
+                in0=sums[:],
+                scalar=weight[:, t, column : column + 1],
+                in1=running[:, t, :],
+                op0=ALU.mult,
+                op1=ALU.add,
+            )
+
+        def flip_hidden(rows, grouped):
+            flipped = flip_banks.tile([P, PACK, P], BF16, tag="flipped")
+            for c in range(PACK):
+                nc.tensor.transpose(flipped[:, c, :], rows[:, c : HIDDEN : PACK], identity_bf16[:])
+            nc.scalar.copy(out=grouped, in_=flipped[:].rearrange("p c r -> p r c"))
+
+        def quantise_hidden(grouped, pool, label, count):
+            codes = pool.tile([P, count], U32, align_bytes=64, name=label + "_codes")
+            scales = pool.tile([P, count], U8, align_bytes=64, name=label + "_scales")
+            nc.vector.quantize_mx(
+                out=codes[:].bitcast(FP8X4), scales=scales[:], in_=grouped[:].rearrange("p r c -> p (r c)")
+            )
+            return codes, scales
+
+        def project(operand, weights, t):
+            codes, scales = operand
+            w_codes, w_scales = weights
+            projected = sum_banks.tile([P, OUTPUTS], F32, tag="sums")
+            nc.tensor.matmul_mx(
+                out=projected[:],
+                lhsT=codes[:].bitcast(FP8X4),
+                lhsT_scale=scales[:],
+                rhs=w_codes[:].bitcast(FP8X4),
+                rhs_scale=w_scales[:],
+                start=True,
+                stop=True,
+            )
+            result = tail_pool.tile([P, OUTPUTS], F32)
+            nc.vector.tensor_tensor(out=result[:], in0=projected[:], in1=bias_all[:, BU], op=ALU.add)
+            nc.sync.dma_start(out=out_tiles[t], in_=result[:])
+
+        def tile_finished_in(q):
+            contexts_done = (q + 1 - CONTEXT_ROUND) * BLOCKS
+            if CONTEXT_ROUND <= q < ROUNDS and contexts_done % CONTEXTS == 0:
+                return contexts_done // CONTEXTS - 1
+            return None
+
+        weights_of = {}
+        hidden_of = {}
+        operands = []
+        for q in range(-1, ROUNDS + 2):
+            coming = q + 1
+            coming_is_weights = coming == WN_ROUND or coming == WC_ROUND
+            coming_is_rows = coming < ROUNDS and not coming_is_weights
+
+            done = tile_finished_in(q - 2)
+            if done is not None:
+                hidden_grouped = tail_pool.tile([P, P, PACK], BF16, align_bytes=64)
+                flip_hidden(hidden_of[done][:], hidden_grouped[:])
+            if coming == WN_ROUND:
+                weights_grouped = flip_weights(coming, "wn")
+            if coming == WC_ROUND:
+                weights_grouped = flip_weights(coming, "wc")
+                wu_grouped = keep.tile([P, OUTPUTS, PACK], BF16, align_bytes=64)
+                for b in range(OUTPUTS // P):
+                    flip_hidden(wu_raw[:, b, :], wu_grouped[:, b * P : (b + 1) * P, :])
+            if coming_is_rows:
+                grouped_blocks = flip_round(coming)
+
+            if done is not None:
+                hidden_operand = quantise_hidden(hidden_grouped, tail_pool, "hidden", P)
+            following = []
+            for j in range(BLOCKS):
+                if coming_is_rows:
+                    following.append(quantise_block(grouped_blocks[j]))
+                if X_ROUND <= q < WC_ROUND:
+                    t = (q - X_ROUND) * BLOCKS + j
+                    add_weighted(multiply_block(operands[j], weights_of["wn"]), t, ONE, running[:, t, :])
+                if CONTEXT_ROUND <= q < ROUNDS:
+                    t, k = divmod((q - CONTEXT_ROUND) * BLOCKS + j, CONTEXTS)
+                    sums = multiply_block(operands[j], weights_of["wc"])
+                    if k < CONTEXTS - 1:
+                        add_weighted(sums, t, k, running[:, t, :])
+                    else:
+                        hidden = tail_pool.tile([P, HIDDEN], BF16)
+                        add_weighted(sums, t, k, hidden[:])
+                        hidden_of[t] = hidden
+            if coming_is_rows:
+                operands = following
+            if coming == WN_ROUND:
+                weights_of["wn"] = quantise_weights(weights_grouped, "wn")
+            if coming == WC_ROUND:
+                weights_of["wc"] = quantise_weights(weights_grouped, "wc")
+                weights_of["wu"] = quantise_hidden(wu_grouped, keep, "wu", OUTPUTS)
+            if done is not None:
+                project(hidden_operand, weights_of["wu"], done)

@@ -27,8 +27,11 @@ CONTEXT_ROUND = WC_ROUND + 1
 ROUNDS = CONTEXT_ROUND + NODE_TILES * CONTEXTS // BLOCKS
 ONE = CONTEXTS
 
-RAW_BUFS = 10 * BLOCKS
-BLOCK_BUFS = 3 * BLOCKS
+PAIR = 2
+RAW_BUFS = 14 * BLOCKS
+SORTED = (1, 3)
+SORT_AHEAD = 2
+PAIR_BUFS = 3 * BLOCKS // PAIR
 
 FLOPS = 2 * NODES * (CONTEXTS + 1) * FEATURES * HIDDEN + 2 * NODES * HIDDEN * OUTPUTS
 
@@ -38,25 +41,26 @@ def tile_nodeembeddinglayer_pa_t_kernel(tc, x, contexts, attn, Wn, bn, Wc, bc, W
     with ExitStack() as stack:
         keep = stack.enter_context(tc.tile_pool(name="keep", bufs=1))
         raw_pool = stack.enter_context(tc.tile_pool(name="raw_pool", bufs=RAW_BUFS))
-        block_pool = stack.enter_context(tc.tile_pool(name="block_pool", bufs=BLOCK_BUFS))
+        pair_pool = stack.enter_context(tc.tile_pool(name="pair_pool", bufs=PAIR_BUFS))
+        sorted_pool = stack.enter_context(tc.tile_pool(name="sorted_pool", bufs=(SORT_AHEAD + 1) * len(SORTED)))
         tail_pool = stack.enter_context(tc.tile_pool(name="tail_pool", bufs=2))
         flip_banks = stack.enter_context(tc.psum_pool(name="flip_banks", bufs=BLOCKS))
         sum_banks = stack.enter_context(tc.psum_pool(name="sum_banks", bufs=BLOCKS))
         stack.enter_context(tc.manual_schedule())
 
         attn_sb = keep.tile([P, NODE_TILES, CONTEXTS], BF16)
-        nc.sync.dma_start(out=attn_sb[:], in_=attn.rearrange("(p t) k -> p t k", t=NODE_TILES))
+        nc.scalar.dma_start(out=attn_sb[:], in_=attn.rearrange("(p t) k -> p t k", t=NODE_TILES))
         BC, BN, BU = slice(0, HIDDEN), slice(HIDDEN, 2 * HIDDEN), slice(2 * HIDDEN, 2 * HIDDEN + OUTPUTS)
         bias_rows = keep.tile([P, 2 * HIDDEN + OUTPUTS], BF16)
-        nc.vector.memset(bias_rows[:], 0.0)
-        nc.sync.dma_start(out=bias_rows[0:1, BC], in_=bc.unsqueeze(0))
-        nc.sync.dma_start(out=bias_rows[0:1, BN], in_=bn.unsqueeze(0))
-        nc.sync.dma_start(out=bias_rows[0:1, BU], in_=bu.unsqueeze(0))
+        nc.vector.memset(bias_rows[:].bitcast(F32), 0.0)
+        nc.scalar.dma_start(out=bias_rows[0:1, BC], in_=bc.unsqueeze(0))
+        nc.scalar.dma_start(out=bias_rows[0:1, BN], in_=bn.unsqueeze(0))
+        nc.scalar.dma_start(out=bias_rows[0:1, BU], in_=bu.unsqueeze(0))
 
         x_blocks = x.rearrange("(p t) f -> t p f", t=NODE_TILES)
         context_blocks = contexts.rearrange("(p t) k f -> (t k) p f", t=NODE_TILES)
-        wn_blocks = Wn.rearrange("(b p) f -> b p f", p=P)
-        wc_blocks = Wc.rearrange("(b p) f -> b p f", p=P)
+        wn_blocks = Wn.rearrange("(p c) f -> c p f", c=PACK)
+        wc_blocks = Wc.rearrange("(p c) f -> c p f", c=PACK)
         sources = (
             [wn_blocks[b] for b in range(BLOCKS)]
             + [x_blocks[t] for t in range(NODE_TILES)]
@@ -66,6 +70,7 @@ def tile_nodeembeddinglayer_pa_t_kernel(tc, x, contexts, attn, Wn, bn, Wc, bc, W
         out_tiles = out.rearrange("(p t) o -> t p o", t=NODE_TILES)
 
         rows_of = {}
+        sorted_of = {}
 
         def load_block(i):
             raw = raw_pool.tile([P, FEATURES], BF16)
@@ -86,12 +91,6 @@ def tile_nodeembeddinglayer_pa_t_kernel(tc, x, contexts, attn, Wn, bn, Wc, bc, W
         ones = keep.tile([P, P], BF16)
         nc.vector.memset(ones[:], 1.0)
 
-        bias_all = keep.tile([P, 2 * HIDDEN + OUTPUTS], F32)
-        for cols, width in ((BC, HIDDEN), (BN, HIDDEN), (BU, OUTPUTS)):
-            spread = sum_banks.tile([P, width], F32, tag="sums")
-            nc.tensor.matmul(out=spread[:], lhsT=ones[:], rhs=bias_rows[:, cols], start=True, stop=True)
-            nc.scalar.copy(out=bias_all[:, cols], in_=spread[:])
-
         weight = keep.tile([P, NODE_TILES, CONTEXTS + 1], F32)
         nc.vector.memset(weight[:], 1.0)
         nc.vector.tensor_scalar_mul(out=weight[:, :, 0:CONTEXTS], in0=attn_sb[:], scalar1=1.0 / CONTEXTS)
@@ -99,8 +98,25 @@ def tile_nodeembeddinglayer_pa_t_kernel(tc, x, contexts, attn, Wn, bn, Wc, bc, W
         nc.vector.tensor_reduce(
             out=weight_sum[:], in_=weight[:, :, 0:CONTEXTS], axis=mybir.AxisListType.X, op=ALU.add
         )
+
+        bias_all = keep.tile([P, 2 * HIDDEN + OUTPUTS], F32)
+
+        def spread_biases(biases):
+            for cols in biases:
+                width = cols.stop - cols.start
+                spread = sum_banks.tile([P, width], F32, tag="sums")
+                nc.tensor.matmul(out=spread[:], lhsT=ones[:], rhs=bias_rows[:, cols], start=True, stop=True)
+                if width == HIDDEN:
+                    nc.vector.tensor_copy(
+                        out=bias_all[:, cols].rearrange("p (c r) -> p c r", c=PACK),
+                        in_=spread[:].rearrange("p (r c) -> p c r", c=PACK),
+                    )
+                else:
+                    nc.vector.tensor_copy(out=bias_all[:, cols], in_=spread[:])
+
         running = keep.tile([P, NODE_TILES, HIDDEN], F32)
-        for t in range(NODE_TILES):
+
+        def start_running(t):
             nc.vector.scalar_tensor_tensor(
                 out=running[:, t, :],
                 in0=bias_all[:, BC],
@@ -115,33 +131,45 @@ def tile_nodeembeddinglayer_pa_t_kernel(tc, x, contexts, attn, Wn, bn, Wc, bc, W
             flipped = flip_banks.tile([P, WORD_PIECES, P], F32, tag="flipped")
             for g in range(PASSES):
                 for u in range(2):
-                    piece = words[:, 2 * P * g + u : 2 * P * (g + 1) : 2]
+                    if i in sorted_of:
+                        piece = sorted_of[i][:, 2 * g + u, :]
+                    else:
+                        piece = words[:, 2 * P * g + u : 2 * P * (g + 1) : 2]
                     nc.tensor.transpose(flipped[:, 2 * g + u, :], piece, identity_f32[:])
             nc.scalar.copy(out=grouped_words, in_=flipped[:].rearrange("p (g u) r -> p g r u", u=2))
             if i + RAW_BUFS < len(sources):
                 load_block(i + RAW_BUFS)
 
-        def flip_round(q):
-            grouped_blocks = []
-            for j in range(BLOCKS):
-                grouped = block_pool.tile([P, PASSES * P * PACK], BF16, align_bytes=64)
-                flip_block(
-                    q * BLOCKS + j,
-                    grouped[:].bitcast(F32).rearrange("p (g r u) -> p g r u", g=PASSES, u=2),
-                )
-                grouped_blocks.append(grouped)
-            return grouped_blocks
+        def sort_words(i):
+            ordered = sorted_pool.tile([P, WORD_PIECES, P], F32)
+            nc.scalar.copy(
+                out=ordered[:].rearrange("p (g u) m -> p g u m", u=2),
+                in_=rows_of[i][:].bitcast(F32).rearrange("p (g m u) -> p g u m", g=PASSES, u=2),
+            )
+            sorted_of[i] = ordered
 
-        def quantise_block(grouped):
-            codes = block_pool.tile([P, PASSES * P], U32, align_bytes=64)
-            scales = block_pool.tile([P, PASSES * P], U8, align_bytes=64)
+        def flip_round(q):
+            pairs = []
+            for first in range(0, BLOCKS, PAIR):
+                grouped = pair_pool.tile([P, PAIR * PASSES * P * PACK], BF16, align_bytes=64)
+                words = grouped[:].bitcast(F32).rearrange("p (j g r u) -> p j g r u", j=PAIR, g=PASSES, u=2)
+                for j in range(PAIR):
+                    flip_block(q * BLOCKS + first + j, words[:, j])
+                pairs.append(grouped)
+            return pairs
+
+        def quantise_pair(grouped):
+            codes = pair_pool.tile([P, PAIR * PASSES * P], U32, align_bytes=64)
+            scales = pair_pool.tile([P, PAIR * PASSES * P], U8, align_bytes=64)
             nc.vector.quantize_mx(out=codes[:].bitcast(FP8X4), scales=scales[:], in_=grouped[:])
             return codes, scales
 
-        def flip_weights(q, label):
+        def flip_weights(q, label, biases):
             grouped = keep.tile([P, PASSES * HIDDEN * PACK], BF16, align_bytes=64, name=label + "_grouped")
             by_block = grouped[:].bitcast(F32).rearrange("p (g b r u) -> p b g r u", g=PASSES, b=BLOCKS, u=2)
             for b in range(BLOCKS):
+                if b == BLOCKS - 1:
+                    spread_biases(biases)
                 flip_block(q * BLOCKS + b, by_block[:, b])
             return grouped
 
@@ -151,12 +179,13 @@ def tile_nodeembeddinglayer_pa_t_kernel(tc, x, contexts, attn, Wn, bn, Wc, bc, W
             nc.vector.quantize_mx(out=codes[:].bitcast(FP8X4), scales=scales[:], in_=grouped[:])
             return codes, scales
 
-        def multiply_block(operand, weights):
-            codes, scales = operand
+        def multiply_block(pairs, j, weights):
+            codes, scales = pairs[j // PAIR]
             w_codes, w_scales = weights
             sums = sum_banks.tile([P, HIDDEN], F32, tag="sums")
             for g in range(PASSES):
-                rows = slice(g * P, (g + 1) * P)
+                first = (j % PAIR * PASSES + g) * P
+                rows = slice(first, first + P)
                 hidden_cols = slice(g * HIDDEN, (g + 1) * HIDDEN)
                 nc.tensor.matmul_mx(
                     out=sums[:],
@@ -182,8 +211,19 @@ def tile_nodeembeddinglayer_pa_t_kernel(tc, x, contexts, attn, Wn, bn, Wc, bc, W
         def flip_hidden(rows, grouped):
             flipped = flip_banks.tile([P, PACK, P], BF16, tag="flipped")
             for c in range(PACK):
-                nc.tensor.transpose(flipped[:, c, :], rows[:, c : HIDDEN : PACK], identity_bf16[:])
+                nc.tensor.transpose(flipped[:, c, :], rows[:, c * P : (c + 1) * P], identity_bf16[:])
             nc.scalar.copy(out=grouped, in_=flipped[:].rearrange("p c r -> p r c"))
+
+        def flip_output_weights(grouped):
+            flipped = flip_banks.tile([P, OUTPUTS // P, 2, P], F32, tag="flipped")
+            for b in range(OUTPUTS // P):
+                words = wu_raw[:, b, :].bitcast(F32)
+                for u in range(2):
+                    nc.tensor.transpose(flipped[:, b, u, :], words[:, u : HIDDEN // 2 : 2], identity_f32[:])
+            nc.scalar.copy(
+                out=grouped[:].rearrange("p o c -> p (o c)").bitcast(F32).rearrange("p (b o u) -> p b o u", u=2, o=P),
+                in_=flipped[:].rearrange("p b u o -> p b o u"),
+            )
 
         def quantise_hidden(grouped, pool, label, count):
             codes = pool.tile([P, count], U32, align_bytes=64, name=label + "_codes")
@@ -229,27 +269,31 @@ def tile_nodeembeddinglayer_pa_t_kernel(tc, x, contexts, attn, Wn, bn, Wc, bc, W
                 hidden_grouped = tail_pool.tile([P, P, PACK], BF16, align_bytes=64)
                 flip_hidden(hidden_of[done][:], hidden_grouped[:])
             if coming == WN_ROUND:
-                weights_grouped = flip_weights(coming, "wn")
+                weights_grouped = flip_weights(coming, "wn", (BC, BN))
             if coming == WC_ROUND:
-                weights_grouped = flip_weights(coming, "wc")
+                weights_grouped = flip_weights(coming, "wc", (BU,))
                 wu_grouped = keep.tile([P, OUTPUTS, PACK], BF16, align_bytes=64)
-                for b in range(OUTPUTS // P):
-                    flip_hidden(wu_raw[:, b, :], wu_grouped[:, b * P : (b + 1) * P, :])
+                flip_output_weights(wu_grouped)
             if coming_is_rows:
-                grouped_blocks = flip_round(coming)
+                grouped_pairs = flip_round(coming)
+            if CONTEXT_ROUND <= coming + SORT_AHEAD < ROUNDS:
+                for j in SORTED:
+                    sort_words((coming + SORT_AHEAD) * BLOCKS + j)
 
             if done is not None:
                 hidden_operand = quantise_hidden(hidden_grouped, tail_pool, "hidden", P)
             following = []
             for j in range(BLOCKS):
-                if coming_is_rows:
-                    following.append(quantise_block(grouped_blocks[j]))
+                if coming_is_rows and j < BLOCKS // PAIR:
+                    following.append(quantise_pair(grouped_pairs[j]))
+                if X_ROUND <= coming < WC_ROUND:
+                    start_running((coming - X_ROUND) * BLOCKS + j)
                 if X_ROUND <= q < WC_ROUND:
                     t = (q - X_ROUND) * BLOCKS + j
-                    add_weighted(multiply_block(operands[j], weights_of["wn"]), t, ONE, running[:, t, :])
+                    add_weighted(multiply_block(operands, j, weights_of["wn"]), t, ONE, running[:, t, :])
                 if CONTEXT_ROUND <= q < ROUNDS:
                     t, k = divmod((q - CONTEXT_ROUND) * BLOCKS + j, CONTEXTS)
-                    sums = multiply_block(operands[j], weights_of["wc"])
+                    sums = multiply_block(operands, j, weights_of["wc"])
                     if k < CONTEXTS - 1:
                         add_weighted(sums, t, k, running[:, t, :])
                     else:

@@ -20,18 +20,32 @@ PASSES = FEATURES // K_PASS
 WORD_PIECES = FEATURES // 2 // P
 
 BLOCKS = 4
-WN_ROUND = 0
-X_ROUND = 1
-WC_ROUND = X_ROUND + NODE_TILES // BLOCKS
-CONTEXT_ROUND = WC_ROUND + 1
-ROUNDS = CONTEXT_ROUND + NODE_TILES * CONTEXTS // BLOCKS
+HALF = CONTEXTS // 2
 ONE = CONTEXTS
+WN, WC = "wn", "wc"
 
 PAIR = 2
 RAW_BUFS = 14 * BLOCKS
 SORTED = (1, 3)
 SORT_AHEAD = 2
 PAIR_BUFS = 3 * BLOCKS // PAIR
+
+
+def plan_rounds():
+    def take_turns(a, b):
+        return [block for pair in zip(a, b) for block in pair]
+
+    def half_of(t, half):
+        return [(t, k) for k in range(half * HALF, (half + 1) * HALF)]
+
+    early_x = [(t, ONE) for t in range(BLOCKS)]
+    late_x = [(t, ONE) for t in range(BLOCKS, NODE_TILES)]
+    mixed = take_turns(half_of(0, 0), late_x)
+    for t in range(NODE_TILES - 1):
+        mixed.extend(take_turns(half_of(t, 1), half_of(t + 1, 0)))
+    mixed.extend(half_of(NODE_TILES - 1, 1))
+    return [WN, early_x, WC] + [mixed[i : i + BLOCKS] for i in range(0, len(mixed), BLOCKS)]
+
 
 FLOPS = 2 * NODES * (CONTEXTS + 1) * FEATURES * HIDDEN + 2 * NODES * HIDDEN * OUTPUTS
 
@@ -61,12 +75,14 @@ def tile_nodeembeddinglayer_pa_t_kernel(tc, x, contexts, attn, Wn, bn, Wc, bc, W
         context_blocks = contexts.rearrange("(p t) k f -> (t k) p f", t=NODE_TILES)
         wn_blocks = Wn.rearrange("(p c) f -> c p f", c=PACK)
         wc_blocks = Wc.rearrange("(p c) f -> c p f", c=PACK)
-        sources = (
-            [wn_blocks[b] for b in range(BLOCKS)]
-            + [x_blocks[t] for t in range(NODE_TILES)]
-            + [wc_blocks[b] for b in range(BLOCKS)]
-            + [context_blocks[c] for c in range(NODE_TILES * CONTEXTS)]
-        )
+        rounds = plan_rounds()
+        sources = []
+        for blocks in rounds:
+            if blocks == WN or blocks == WC:
+                weight_blocks = wn_blocks if blocks == WN else wc_blocks
+                sources.extend([weight_blocks[b] for b in range(BLOCKS)])
+            else:
+                sources.extend([x_blocks[t] if k == ONE else context_blocks[t * CONTEXTS + k] for t, k in blocks])
         out_tiles = out.rearrange("(p t) o -> t p o", t=NODE_TILES)
 
         rows_of = {}
@@ -77,11 +93,12 @@ def tile_nodeembeddinglayer_pa_t_kernel(tc, x, contexts, attn, Wn, bn, Wc, bc, W
             nc.sync.dma_start(out=raw[:], in_=sources[i])
             rows_of[i] = raw
 
-        for i in range(CONTEXT_ROUND * BLOCKS):
+        before_wu = (rounds.index(WC) + 1) * BLOCKS
+        for i in range(before_wu):
             load_block(i)
         wu_raw = keep.tile([P, OUTPUTS // P, HIDDEN], BF16)
         nc.sync.dma_start(out=wu_raw[:], in_=Wu.rearrange("(b p) h -> p b h", p=P))
-        for i in range(CONTEXT_ROUND * BLOCKS, RAW_BUFS):
+        for i in range(before_wu, RAW_BUFS):
             load_block(i)
 
         identity_f32 = keep.tile([P, P], F32)
@@ -250,62 +267,56 @@ def tile_nodeembeddinglayer_pa_t_kernel(tc, x, contexts, attn, Wn, bn, Wc, bc, W
             nc.vector.tensor_tensor(out=result[:], in0=projected[:], in1=bias_all[:, BU], op=ALU.add)
             nc.sync.dma_start(out=out_tiles[t], in_=result[:])
 
-        def tile_finished_in(q):
-            contexts_done = (q + 1 - CONTEXT_ROUND) * BLOCKS
-            if CONTEXT_ROUND <= q < ROUNDS and contexts_done % CONTEXTS == 0:
-                return contexts_done // CONTEXTS - 1
-            return None
+        def blocks_of(q):
+            return rounds[q] if 0 <= q < len(rounds) and rounds[q] != WN and rounds[q] != WC else []
 
         weights_of = {}
         hidden_of = {}
         operands = []
-        for q in range(-1, ROUNDS + 2):
-            coming = q + 1
-            coming_is_weights = coming == WN_ROUND or coming == WC_ROUND
-            coming_is_rows = coming < ROUNDS and not coming_is_weights
+        for q in range(-1, len(rounds) + 2):
+            coming = rounds[q + 1] if q + 1 < len(rounds) else None
+            coming_rows = blocks_of(q + 1)
 
-            done = tile_finished_in(q - 2)
-            if done is not None:
+            done = [t for t, k in blocks_of(q - 2) if k == CONTEXTS - 1]
+            for t in done:
                 hidden_grouped = tail_pool.tile([P, P, PACK], BF16, align_bytes=64)
-                flip_hidden(hidden_of[done][:], hidden_grouped[:])
-            if coming == WN_ROUND:
-                weights_grouped = flip_weights(coming, "wn", (BC, BN))
-            if coming == WC_ROUND:
-                weights_grouped = flip_weights(coming, "wc", (BU,))
+                flip_hidden(hidden_of[t][:], hidden_grouped[:])
+            if coming == WN:
+                weights_grouped = flip_weights(q + 1, WN, (BC, BN))
+            if coming == WC:
+                weights_grouped = flip_weights(q + 1, WC, (BU,))
                 wu_grouped = keep.tile([P, OUTPUTS, PACK], BF16, align_bytes=64)
                 flip_output_weights(wu_grouped)
-            if coming_is_rows:
-                grouped_pairs = flip_round(coming)
-            if CONTEXT_ROUND <= coming + SORT_AHEAD < ROUNDS:
+            if coming_rows:
+                grouped_pairs = flip_round(q + 1)
+            if q + 1 + SORT_AHEAD > rounds.index(WC) and blocks_of(q + 1 + SORT_AHEAD):
                 for j in SORTED:
-                    sort_words((coming + SORT_AHEAD) * BLOCKS + j)
+                    sort_words((q + 1 + SORT_AHEAD) * BLOCKS + j)
 
-            if done is not None:
+            for t in done:
                 hidden_operand = quantise_hidden(hidden_grouped, tail_pool, "hidden", P)
             following = []
+            multiplied = blocks_of(q)
             for j in range(BLOCKS):
-                if coming_is_rows and j < BLOCKS // PAIR:
+                if coming_rows and j < BLOCKS // PAIR:
                     following.append(quantise_pair(grouped_pairs[j]))
-                if X_ROUND <= coming < WC_ROUND:
-                    start_running((coming - X_ROUND) * BLOCKS + j)
-                if X_ROUND <= q < WC_ROUND:
-                    t = (q - X_ROUND) * BLOCKS + j
-                    add_weighted(multiply_block(operands, j, weights_of["wn"]), t, ONE, running[:, t, :])
-                if CONTEXT_ROUND <= q < ROUNDS:
-                    t, k = divmod((q - CONTEXT_ROUND) * BLOCKS + j, CONTEXTS)
-                    sums = multiply_block(operands, j, weights_of["wc"])
-                    if k < CONTEXTS - 1:
-                        add_weighted(sums, t, k, running[:, t, :])
-                    else:
+                if coming_rows and coming_rows[j][1] == ONE:
+                    start_running(coming_rows[j][0])
+                if multiplied:
+                    t, k = multiplied[j]
+                    sums = multiply_block(operands, j, weights_of[WN if k == ONE else WC])
+                    if k == CONTEXTS - 1:
                         hidden = tail_pool.tile([P, HIDDEN], BF16)
                         add_weighted(sums, t, k, hidden[:])
                         hidden_of[t] = hidden
-            if coming_is_rows:
+                    else:
+                        add_weighted(sums, t, k, running[:, t, :])
+            if coming_rows:
                 operands = following
-            if coming == WN_ROUND:
-                weights_of["wn"] = quantise_weights(weights_grouped, "wn")
-            if coming == WC_ROUND:
-                weights_of["wc"] = quantise_weights(weights_grouped, "wc")
+            if coming == WN:
+                weights_of[WN] = quantise_weights(weights_grouped, WN)
+            if coming == WC:
+                weights_of[WC] = quantise_weights(weights_grouped, WC)
                 weights_of["wu"] = quantise_hidden(wu_grouped, keep, "wu", OUTPUTS)
-            if done is not None:
-                project(hidden_operand, weights_of["wu"], done)
+            for t in done:
+                project(hidden_operand, weights_of["wu"], t)

@@ -28,23 +28,22 @@ PAIR = 2
 RAW_BUFS = 14 * BLOCKS
 SORTED = (1, 3)
 SORT_AHEAD = 2
+FIRST_ROWS = 1
+FIRST_SORTED = 5
 PAIR_BUFS = 3 * BLOCKS // PAIR
 
 
 def plan_rounds():
-    def take_turns(a, b):
-        return [block for pair in zip(a, b) for block in pair]
-
-    def half_of(t, half):
-        return [(t, k) for k in range(half * HALF, (half + 1) * HALF)]
-
-    early_x = [(t, ONE) for t in range(BLOCKS)]
-    late_x = [(t, ONE) for t in range(BLOCKS, NODE_TILES)]
-    mixed = take_turns(half_of(0, 0), late_x)
+    first_half = [[(t, k) for k in range(HALF)] for t in range(NODE_TILES)]
+    second_half = [[(t, k) for k in [ONE] + list(range(HALF, CONTEXTS))] for t in range(NODE_TILES)]
+    blocks = list(first_half[0])
     for t in range(NODE_TILES - 1):
-        mixed.extend(take_turns(half_of(t, 1), half_of(t + 1, 0)))
-    mixed.extend(half_of(NODE_TILES - 1, 1))
-    return [WN, early_x, WC] + [mixed[i : i + BLOCKS] for i in range(0, len(mixed), BLOCKS)]
+        for i in range(len(second_half[t])):
+            blocks.append(second_half[t][i])
+            blocks.extend(first_half[t + 1][i : i + 1])
+    blocks.extend(second_half[NODE_TILES - 1])
+    row_rounds = [blocks[i : i + BLOCKS] for i in range(0, len(blocks), BLOCKS)]
+    return [WC, row_rounds[0], WN] + row_rounds[1:]
 
 
 FLOPS = 2 * NODES * (CONTEXTS + 1) * FEATURES * HIDDEN + 2 * NODES * HIDDEN * OUTPUTS
@@ -93,7 +92,7 @@ def tile_nodeembeddinglayer_pa_t_kernel(tc, x, contexts, attn, Wn, bn, Wc, bc, W
             nc.sync.dma_start(out=raw[:], in_=sources[i])
             rows_of[i] = raw
 
-        before_wu = (rounds.index(WC) + 1) * BLOCKS
+        before_wu = (rounds.index(WN) + 1) * BLOCKS
         for i in range(before_wu):
             load_block(i)
         wu_raw = keep.tile([P, OUTPUTS // P, HIDDEN], BF16)
@@ -134,16 +133,27 @@ def tile_nodeembeddinglayer_pa_t_kernel(tc, x, contexts, attn, Wn, bn, Wc, bc, W
         running = keep.tile([P, NODE_TILES, HIDDEN], F32)
 
         def start_running(t):
-            nc.vector.scalar_tensor_tensor(
-                out=running[:, t, :],
-                in0=bias_all[:, BC],
-                scalar=weight_sum[:, t : t + 1],
-                in1=bias_all[:, BN],
-                op0=ALU.mult,
-                op1=ALU.add,
-            )
+            if t == 0:
+                nc.vector.scalar_tensor_tensor(
+                    out=running[:, t, :],
+                    in0=bias_all[:, BC],
+                    scalar=weight_sum[:, t : t + 1],
+                    in1=bias_all[:, BN],
+                    op0=ALU.mult,
+                    op1=ALU.add,
+                )
+            else:
+                nc.gpsimd.tensor_scalar(
+                    out=running[:, t, :],
+                    in0=bias_all[:, BC],
+                    scalar1=weight_sum[:, t : t + 1],
+                    scalar2=0.0,
+                    op0=ALU.mult,
+                    op1=ALU.add,
+                )
+                nc.gpsimd.tensor_tensor(out=running[:, t, :], in0=running[:, t, :], in1=bias_all[:, BN], op=ALU.add)
 
-        def flip_block(i, grouped_words):
+        def flip_block(i, grouped_words, copy=nc.scalar.copy):
             words = rows_of[i][:].bitcast(F32)
             flipped = flip_banks.tile([P, WORD_PIECES, P], F32, tag="flipped")
             for g in range(PASSES):
@@ -153,7 +163,7 @@ def tile_nodeembeddinglayer_pa_t_kernel(tc, x, contexts, attn, Wn, bn, Wc, bc, W
                     else:
                         piece = words[:, 2 * P * g + u : 2 * P * (g + 1) : 2]
                     nc.tensor.transpose(flipped[:, 2 * g + u, :], piece, identity_f32[:])
-            nc.scalar.copy(out=grouped_words, in_=flipped[:].rearrange("p (g u) r -> p g r u", u=2))
+            copy(out=grouped_words, in_=flipped[:].rearrange("p (g u) r -> p g r u", u=2))
             if i + RAW_BUFS < len(sources):
                 load_block(i + RAW_BUFS)
 
@@ -181,13 +191,11 @@ def tile_nodeembeddinglayer_pa_t_kernel(tc, x, contexts, attn, Wn, bn, Wc, bc, W
             nc.vector.quantize_mx(out=codes[:].bitcast(FP8X4), scales=scales[:], in_=grouped[:])
             return codes, scales
 
-        def flip_weights(q, label, biases):
+        def flip_weights(q, label):
             grouped = keep.tile([P, PASSES * HIDDEN * PACK], BF16, align_bytes=64, name=label + "_grouped")
             by_block = grouped[:].bitcast(F32).rearrange("p (g b r u) -> p b g r u", g=PASSES, b=BLOCKS, u=2)
             for b in range(BLOCKS):
-                if b == BLOCKS - 1:
-                    spread_biases(biases)
-                flip_block(q * BLOCKS + b, by_block[:, b])
+                flip_block(q * BLOCKS + b, by_block[:, b], (nc.scalar.copy, nc.vector.tensor_copy)[b % 2])
             return grouped
 
         def quantise_weights(grouped, label):
@@ -264,7 +272,12 @@ def tile_nodeembeddinglayer_pa_t_kernel(tc, x, contexts, attn, Wn, bn, Wc, bc, W
                 stop=True,
             )
             result = tail_pool.tile([P, OUTPUTS], F32)
-            nc.vector.tensor_tensor(out=result[:], in0=projected[:], in1=bias_all[:, BU], op=ALU.add)
+            if t == NODE_TILES - 1:
+                nc.vector.tensor_tensor(out=result[:], in0=projected[:], in1=bias_all[:, BU], op=ALU.add)
+            else:
+                unbiased = tail_pool.tile([P, OUTPUTS], F32)
+                nc.scalar.copy(out=unbiased[:], in_=projected[:])
+                nc.gpsimd.tensor_tensor(out=result[:], in0=unbiased[:], in1=bias_all[:, BU], op=ALU.add)
             nc.sync.dma_start(out=out_tiles[t], in_=result[:])
 
         def blocks_of(q):
@@ -277,19 +290,19 @@ def tile_nodeembeddinglayer_pa_t_kernel(tc, x, contexts, attn, Wn, bn, Wc, bc, W
             coming = rounds[q + 1] if q + 1 < len(rounds) else None
             coming_rows = blocks_of(q + 1)
 
-            done = [t for t, k in blocks_of(q - 2) if k == CONTEXTS - 1]
+            done = [t for t, k in blocks_of(q - 2) if k == CONTEXTS - 1 and q != len(rounds)]
+            early = [t for t, k in blocks_of(q - 1) if k == CONTEXTS - 1 and q == len(rounds) - 1]
             for t in done:
                 hidden_grouped = tail_pool.tile([P, P, PACK], BF16, align_bytes=64)
                 flip_hidden(hidden_of[t][:], hidden_grouped[:])
+            if coming == WN or coming == WC:
+                weights_grouped = flip_weights(q + 1, coming)
             if coming == WN:
-                weights_grouped = flip_weights(q + 1, WN, (BC, BN))
-            if coming == WC:
-                weights_grouped = flip_weights(q + 1, WC, (BU,))
                 wu_grouped = keep.tile([P, OUTPUTS, PACK], BF16, align_bytes=64)
                 flip_output_weights(wu_grouped)
             if coming_rows:
                 grouped_pairs = flip_round(q + 1)
-            if q + 1 + SORT_AHEAD > rounds.index(WC) and blocks_of(q + 1 + SORT_AHEAD):
+            if q + 1 + SORT_AHEAD >= FIRST_SORTED and blocks_of(q + 1 + SORT_AHEAD):
                 for j in SORTED:
                     sort_words((q + 1 + SORT_AHEAD) * BLOCKS + j)
 
@@ -300,8 +313,10 @@ def tile_nodeembeddinglayer_pa_t_kernel(tc, x, contexts, attn, Wn, bn, Wc, bc, W
             for j in range(BLOCKS):
                 if coming_rows and j < BLOCKS // PAIR:
                     following.append(quantise_pair(grouped_pairs[j]))
-                if coming_rows and coming_rows[j][1] == ONE:
-                    start_running(coming_rows[j][0])
+                    if q + 1 == FIRST_ROWS and j == 0:
+                        spread_biases((BC, BN))
+                        for t in range(NODE_TILES):
+                            start_running(t)
                 if multiplied:
                     t, k = multiplied[j]
                     sums = multiply_block(operands, j, weights_of[WN if k == ONE else WC])
@@ -311,12 +326,19 @@ def tile_nodeembeddinglayer_pa_t_kernel(tc, x, contexts, attn, Wn, bn, Wc, bc, W
                         hidden_of[t] = hidden
                     else:
                         add_weighted(sums, t, k, running[:, t, :])
+                if j == PAIR - 1:
+                    for t in early:
+                        hidden_grouped = tail_pool.tile([P, P, PACK], BF16, align_bytes=64)
+                        flip_hidden(hidden_of[t][:], hidden_grouped[:])
+                if j == BLOCKS - 2:
+                    for t in early:
+                        hidden_operand = quantise_hidden(hidden_grouped, tail_pool, "hidden", P)
             if coming_rows:
                 operands = following
+            if coming == WN or coming == WC:
+                weights_of[coming] = quantise_weights(weights_grouped, coming)
             if coming == WN:
-                weights_of[WN] = quantise_weights(weights_grouped, WN)
-            if coming == WC:
-                weights_of[WC] = quantise_weights(weights_grouped, WC)
                 weights_of["wu"] = quantise_hidden(wu_grouped, keep, "wu", OUTPUTS)
-            for t in done:
+                spread_biases((BU,))
+            for t in done + early:
                 project(hidden_operand, weights_of["wu"], t)

@@ -25,11 +25,12 @@ ONE = CONTEXTS
 WN, WC = "wn", "wc"
 
 PAIR = 2
-RAW_BUFS = 14 * BLOCKS
-SORTED = (1, 3)
+RAW_BUFS = 12 * BLOCKS
 SORT_AHEAD = 2
+SORTERS = ("scalar", "scalar", "gpsimd", "gpsimd")
 FIRST_ROWS = 1
-FIRST_SORTED = 5
+FIRST_SORTED = 4
+QUANTISE_BEFORE = (2, 3)
 PAIR_BUFS = 3 * BLOCKS // PAIR
 
 
@@ -55,7 +56,7 @@ def tile_nodeembeddinglayer_pa_t_kernel(tc, x, contexts, attn, Wn, bn, Wc, bc, W
         keep = stack.enter_context(tc.tile_pool(name="keep", bufs=1))
         raw_pool = stack.enter_context(tc.tile_pool(name="raw_pool", bufs=RAW_BUFS))
         pair_pool = stack.enter_context(tc.tile_pool(name="pair_pool", bufs=PAIR_BUFS))
-        sorted_pool = stack.enter_context(tc.tile_pool(name="sorted_pool", bufs=(SORT_AHEAD + 1) * len(SORTED)))
+        sorted_pool = stack.enter_context(tc.tile_pool(name="sorted_pool", bufs=(SORT_AHEAD + 1) * BLOCKS))
         tail_pool = stack.enter_context(tc.tile_pool(name="tail_pool", bufs=2))
         flip_banks = stack.enter_context(tc.psum_pool(name="flip_banks", bufs=BLOCKS))
         sum_banks = stack.enter_context(tc.psum_pool(name="sum_banks", bufs=BLOCKS))
@@ -167,9 +168,11 @@ def tile_nodeembeddinglayer_pa_t_kernel(tc, x, contexts, attn, Wn, bn, Wc, bc, W
             if i + RAW_BUFS < len(sources):
                 load_block(i + RAW_BUFS)
 
-        def sort_words(i):
+        sort_copy = {"scalar": nc.scalar.copy, "gpsimd": nc.gpsimd.tensor_copy, "vector": nc.vector.tensor_copy}
+
+        def sort_words(i, copy):
             ordered = sorted_pool.tile([P, WORD_PIECES, P], F32)
-            nc.scalar.copy(
+            copy(
                 out=ordered[:].rearrange("p (g u) m -> p g u m", u=2),
                 in_=rows_of[i][:].bitcast(F32).rearrange("p (g m u) -> p g u m", g=PASSES, u=2),
             )
@@ -261,7 +264,7 @@ def tile_nodeembeddinglayer_pa_t_kernel(tc, x, contexts, attn, Wn, bn, Wc, bc, W
         def project(operand, weights, t):
             codes, scales = operand
             w_codes, w_scales = weights
-            projected = sum_banks.tile([P, OUTPUTS], F32, tag="sums")
+            projected = flip_banks.tile([P, OUTPUTS], F32, tag="flipped")
             nc.tensor.matmul_mx(
                 out=projected[:],
                 lhsT=codes[:].bitcast(FP8X4),
@@ -302,21 +305,24 @@ def tile_nodeembeddinglayer_pa_t_kernel(tc, x, contexts, attn, Wn, bn, Wc, bc, W
                 flip_output_weights(wu_grouped)
             if coming_rows:
                 grouped_pairs = flip_round(q + 1)
-            if q + 1 + SORT_AHEAD >= FIRST_SORTED and blocks_of(q + 1 + SORT_AHEAD):
-                for j in SORTED:
-                    sort_words((q + 1 + SORT_AHEAD) * BLOCKS + j)
+            for t, k in coming_rows:
+                if k == 0 and t > 0:
+                    start_running(t)
+            to_sort = q + 1 + SORT_AHEAD
+            if FIRST_SORTED <= to_sort < len(rounds):
+                for j in range(BLOCKS):
+                    sort_words(to_sort * BLOCKS + j, sort_copy[SORTERS[j]])
 
             for t in done:
                 hidden_operand = quantise_hidden(hidden_grouped, tail_pool, "hidden", P)
             following = []
             multiplied = blocks_of(q)
             for j in range(BLOCKS):
-                if coming_rows and j < BLOCKS // PAIR:
-                    following.append(quantise_pair(grouped_pairs[j]))
-                    if q + 1 == FIRST_ROWS and j == 0:
+                if coming_rows and j in QUANTISE_BEFORE:
+                    following.append(quantise_pair(grouped_pairs[len(following)]))
+                    if q + 1 == FIRST_ROWS and len(following) == 1:
                         spread_biases((BC, BN))
-                        for t in range(NODE_TILES):
-                            start_running(t)
+                        start_running(0)
                 if multiplied:
                     t, k = multiplied[j]
                     sums = multiply_block(operands, j, weights_of[WN if k == ONE else WC])

@@ -58,8 +58,7 @@ def tile_nodeembeddinglayer_pa_t_kernel(tc, x, contexts, attn, Wn, bn, Wc, bc, W
         pair_pool = stack.enter_context(tc.tile_pool(name="pair_pool", bufs=PAIR_BUFS))
         sorted_pool = stack.enter_context(tc.tile_pool(name="sorted_pool", bufs=(SORT_AHEAD + 1) * BLOCKS))
         tail_pool = stack.enter_context(tc.tile_pool(name="tail_pool", bufs=2))
-        flip_banks = stack.enter_context(tc.psum_pool(name="flip_banks", bufs=BLOCKS))
-        sum_banks = stack.enter_context(tc.psum_pool(name="sum_banks", bufs=BLOCKS))
+        banks = stack.enter_context(tc.psum_pool(name="banks", bufs=2 * BLOCKS))
         stack.enter_context(tc.manual_schedule())
 
         attn_sb = keep.tile([P, NODE_TILES, CONTEXTS], BF16)
@@ -121,7 +120,7 @@ def tile_nodeembeddinglayer_pa_t_kernel(tc, x, contexts, attn, Wn, bn, Wc, bc, W
         def spread_biases(biases):
             for cols in biases:
                 width = cols.stop - cols.start
-                spread = sum_banks.tile([P, width], F32, tag="sums")
+                spread = banks.tile([P, width], F32, tag="bank")
                 nc.tensor.matmul(out=spread[:], lhsT=ones[:], rhs=bias_rows[:, cols], start=True, stop=True)
                 if width == HIDDEN:
                     nc.vector.tensor_copy(
@@ -134,29 +133,18 @@ def tile_nodeembeddinglayer_pa_t_kernel(tc, x, contexts, attn, Wn, bn, Wc, bc, W
         running = keep.tile([P, NODE_TILES, HIDDEN], F32)
 
         def start_running(t):
-            if t == 0:
-                nc.vector.scalar_tensor_tensor(
-                    out=running[:, t, :],
-                    in0=bias_all[:, BC],
-                    scalar=weight_sum[:, t : t + 1],
-                    in1=bias_all[:, BN],
-                    op0=ALU.mult,
-                    op1=ALU.add,
-                )
-            else:
-                nc.gpsimd.tensor_scalar(
-                    out=running[:, t, :],
-                    in0=bias_all[:, BC],
-                    scalar1=weight_sum[:, t : t + 1],
-                    scalar2=0.0,
-                    op0=ALU.mult,
-                    op1=ALU.add,
-                )
-                nc.gpsimd.tensor_tensor(out=running[:, t, :], in0=running[:, t, :], in1=bias_all[:, BN], op=ALU.add)
+            nc.vector.scalar_tensor_tensor(
+                out=running[:, t, :],
+                in0=bias_all[:, BC],
+                scalar=weight_sum[:, t : t + 1],
+                in1=bias_all[:, BN],
+                op0=ALU.mult,
+                op1=ALU.add,
+            )
 
         def flip_block(i, grouped_words, copy=nc.scalar.copy):
             words = rows_of[i][:].bitcast(F32)
-            flipped = flip_banks.tile([P, WORD_PIECES, P], F32, tag="flipped")
+            flipped = banks.tile([P, WORD_PIECES, P], F32, tag="bank")
             for g in range(PASSES):
                 for u in range(2):
                     if i in sorted_of:
@@ -210,7 +198,7 @@ def tile_nodeembeddinglayer_pa_t_kernel(tc, x, contexts, attn, Wn, bn, Wc, bc, W
         def multiply_block(pairs, j, weights):
             codes, scales = pairs[j // PAIR]
             w_codes, w_scales = weights
-            sums = sum_banks.tile([P, HIDDEN], F32, tag="sums")
+            sums = banks.tile([P, HIDDEN], F32, tag="bank")
             for g in range(PASSES):
                 first = (j % PAIR * PASSES + g) * P
                 rows = slice(first, first + P)
@@ -237,13 +225,15 @@ def tile_nodeembeddinglayer_pa_t_kernel(tc, x, contexts, attn, Wn, bn, Wc, bc, W
             )
 
         def flip_hidden(rows, grouped):
-            flipped = flip_banks.tile([P, PACK, P], BF16, tag="flipped")
+            flipped = banks.tile([P, PACK, P], F32, tag="bank")
             for c in range(PACK):
-                nc.tensor.transpose(flipped[:, c, :], rows[:, c * P : (c + 1) * P], identity_bf16[:])
+                nc.tensor.matmul(
+                    out=flipped[:, c, :], lhsT=rows[:, c * P : (c + 1) * P], rhs=identity_bf16[:], start=True, stop=True
+                )
             nc.scalar.copy(out=grouped, in_=flipped[:].rearrange("p c r -> p r c"))
 
         def flip_output_weights(grouped):
-            flipped = flip_banks.tile([P, OUTPUTS // P, 2, P], F32, tag="flipped")
+            flipped = banks.tile([P, OUTPUTS // P, 2, P], F32, tag="bank")
             for b in range(OUTPUTS // P):
                 words = wu_raw[:, b, :].bitcast(F32)
                 for u in range(2):
@@ -264,7 +254,7 @@ def tile_nodeembeddinglayer_pa_t_kernel(tc, x, contexts, attn, Wn, bn, Wc, bc, W
         def project(operand, weights, t):
             codes, scales = operand
             w_codes, w_scales = weights
-            projected = flip_banks.tile([P, OUTPUTS], F32, tag="flipped")
+            projected = banks.tile([P, OUTPUTS], F32, tag="bank")
             nc.tensor.matmul_mx(
                 out=projected[:],
                 lhsT=codes[:].bitcast(FP8X4),
@@ -305,9 +295,6 @@ def tile_nodeembeddinglayer_pa_t_kernel(tc, x, contexts, attn, Wn, bn, Wc, bc, W
                 flip_output_weights(wu_grouped)
             if coming_rows:
                 grouped_pairs = flip_round(q + 1)
-            for t, k in coming_rows:
-                if k == 0 and t > 0:
-                    start_running(t)
             to_sort = q + 1 + SORT_AHEAD
             if FIRST_SORTED <= to_sort < len(rounds):
                 for j in range(BLOCKS):
@@ -339,6 +326,9 @@ def tile_nodeembeddinglayer_pa_t_kernel(tc, x, contexts, attn, Wn, bn, Wc, bc, W
                 if j == BLOCKS - 2:
                     for t in early:
                         hidden_operand = quantise_hidden(hidden_grouped, tail_pool, "hidden", P)
+            if q == FIRST_ROWS:
+                for t in range(1, NODE_TILES):
+                    start_running(t)
             if coming_rows:
                 operands = following
             if coming == WN or coming == WC:

@@ -36,7 +36,7 @@ PAIR_BUFS = 3 * BLOCKS // PAIR
 
 def plan_rounds():
     first_half = [[(t, k) for k in range(HALF)] for t in range(NODE_TILES)]
-    second_half = [[(t, k) for k in [ONE] + list(range(HALF, CONTEXTS))] for t in range(NODE_TILES)]
+    second_half = [[(t, k) for k in [HALF, HALF + 1, ONE] + list(range(HALF + 2, CONTEXTS))] for t in range(NODE_TILES)]
     blocks = list(first_half[0])
     for t in range(NODE_TILES - 1):
         for i in range(len(second_half[t])):
@@ -182,11 +182,11 @@ def tile_nodeembeddinglayer_pa_t_kernel(tc, x, contexts, attn, Wn, bn, Wc, bc, W
             nc.vector.quantize_mx(out=codes[:].bitcast(FP8X4), scales=scales[:], in_=grouped[:])
             return codes, scales
 
-        def flip_weights(q, label):
+        def flip_weights(q, label, copies):
             grouped = keep.tile([P, PASSES * HIDDEN * PACK], BF16, align_bytes=64, name=label + "_grouped")
             by_block = grouped[:].bitcast(F32).rearrange("p (g b r u) -> p b g r u", g=PASSES, b=BLOCKS, u=2)
             for b in range(BLOCKS):
-                flip_block(q * BLOCKS + b, by_block[:, b], (nc.scalar.copy, nc.vector.tensor_copy)[b % 2])
+                flip_block(q * BLOCKS + b, by_block[:, b], copies[b % len(copies)])
             return grouped
 
         def quantise_weights(grouped, label):
@@ -288,9 +288,10 @@ def tile_nodeembeddinglayer_pa_t_kernel(tc, x, contexts, attn, Wn, bn, Wc, bc, W
             for t in done:
                 hidden_grouped = tail_pool.tile([P, P, PACK], BF16, align_bytes=64)
                 flip_hidden(hidden_of[t][:], hidden_grouped[:])
-            if coming == WN or coming == WC:
-                weights_grouped = flip_weights(q + 1, coming)
+            if coming == WC:
+                weights_grouped = flip_weights(q + 1, coming, (nc.scalar.copy, nc.vector.tensor_copy))
             if coming == WN:
+                weights_grouped = flip_weights(q + 1, coming, (nc.scalar.copy,))
                 wu_grouped = keep.tile([P, OUTPUTS, PACK], BF16, align_bytes=64)
                 flip_output_weights(wu_grouped)
             if coming_rows:
@@ -299,6 +300,10 @@ def tile_nodeembeddinglayer_pa_t_kernel(tc, x, contexts, attn, Wn, bn, Wc, bc, W
             if FIRST_SORTED <= to_sort < len(rounds):
                 for j in range(BLOCKS):
                     sort_words(to_sort * BLOCKS + j, sort_copy[SORTERS[j]])
+
+            if q + 2 == FIRST_SORTED - 1:
+                for j in range(BLOCKS):
+                    sort_words((FIRST_SORTED - 1) * BLOCKS + j, nc.vector.tensor_copy)
 
             for t in done:
                 hidden_operand = quantise_hidden(hidden_grouped, tail_pool, "hidden", P)
@@ -326,14 +331,15 @@ def tile_nodeembeddinglayer_pa_t_kernel(tc, x, contexts, attn, Wn, bn, Wc, bc, W
                 if j == BLOCKS - 2:
                     for t in early:
                         hidden_operand = quantise_hidden(hidden_grouped, tail_pool, "hidden", P)
-            if q == FIRST_ROWS:
-                for t in range(1, NODE_TILES):
+            for t, k in coming_rows:
+                if k == 0 and t > 0:
                     start_running(t)
             if coming_rows:
                 operands = following
-            if coming == WN or coming == WC:
-                weights_of[coming] = quantise_weights(weights_grouped, coming)
-            if coming == WN:
+            if coming == WC:
+                weights_of[WC] = quantise_weights(weights_grouped, WC)
+            if 0 <= q < len(rounds) and rounds[q] == WN:
+                weights_of[WN] = quantise_weights(weights_grouped, WN)
                 weights_of["wu"] = quantise_hidden(wu_grouped, keep, "wu", OUTPUTS)
                 spread_biases((BU,))
             for t in done + early:

@@ -30,7 +30,7 @@ SORT_AHEAD = 2
 SORTERS = ("scalar", "scalar", "gpsimd", "gpsimd")
 FIRST_ROWS = 1
 FIRST_SORTED = 4
-QUANTISE_BEFORE = (2, 3)
+QUANTISE_BEFORE = (1, 2)
 PAIR_BUFS = 3 * BLOCKS // PAIR
 
 
@@ -63,12 +63,10 @@ def tile_nodeembeddinglayer_pa_t_kernel(tc, x, contexts, attn, Wn, bn, Wc, bc, W
 
         attn_sb = keep.tile([P, NODE_TILES, CONTEXTS], BF16)
         nc.scalar.dma_start(out=attn_sb[:], in_=attn.rearrange("(p t) k -> p t k", t=NODE_TILES))
-        BC, BN, BU = slice(0, HIDDEN), slice(HIDDEN, 2 * HIDDEN), slice(2 * HIDDEN, 2 * HIDDEN + OUTPUTS)
-        bias_rows = keep.tile([P, 2 * HIDDEN + OUTPUTS], BF16)
+        bias_rows = keep.tile([P, HIDDEN], BF16)
+        bu_row = keep.tile([P, OUTPUTS], BF16)
         nc.vector.memset(bias_rows[:].bitcast(F32), 0.0)
-        nc.scalar.dma_start(out=bias_rows[0:1, BC], in_=bc.unsqueeze(0))
-        nc.scalar.dma_start(out=bias_rows[0:1, BN], in_=bn.unsqueeze(0))
-        nc.scalar.dma_start(out=bias_rows[0:1, BU], in_=bu.unsqueeze(0))
+        nc.vector.memset(bu_row[:].bitcast(F32), 0.0)
 
         x_blocks = x.rearrange("(p t) f -> t p f", t=NODE_TILES)
         context_blocks = contexts.rearrange("(p t) k f -> (t k) p f", t=NODE_TILES)
@@ -92,8 +90,13 @@ def tile_nodeembeddinglayer_pa_t_kernel(tc, x, contexts, attn, Wn, bn, Wc, bc, W
             nc.sync.dma_start(out=raw[:], in_=sources[i])
             rows_of[i] = raw
 
-        before_wu = (rounds.index(WN) + 1) * BLOCKS
-        for i in range(before_wu):
+        before_biases, before_wu = rounds.index(WN) * BLOCKS, (rounds.index(WN) + 1) * BLOCKS
+        for i in range(before_biases):
+            load_block(i)
+        nc.sync.dma_start(out=bias_rows[0:CONTEXTS, :], in_=bc.partition_broadcast(CONTEXTS))
+        nc.sync.dma_start(out=bias_rows[ONE : ONE + 1, :], in_=bn.unsqueeze(0))
+        nc.sync.dma_start(out=bu_row[0:1, :], in_=bu.unsqueeze(0))
+        for i in range(before_biases, before_wu):
             load_block(i)
         wu_raw = keep.tile([P, OUTPUTS // P, HIDDEN], BF16)
         nc.sync.dma_start(out=wu_raw[:], in_=Wu.rearrange("(b p) h -> p b h", p=P))
@@ -110,37 +113,35 @@ def tile_nodeembeddinglayer_pa_t_kernel(tc, x, contexts, attn, Wn, bn, Wc, bc, W
         weight = keep.tile([P, NODE_TILES, CONTEXTS + 1], F32)
         nc.vector.memset(weight[:], 1.0)
         nc.vector.tensor_scalar_mul(out=weight[:, :, 0:CONTEXTS], in0=attn_sb[:], scalar1=1.0 / CONTEXTS)
-        weight_sum = keep.tile([P, NODE_TILES], F32)
-        nc.vector.tensor_reduce(
-            out=weight_sum[:], in_=weight[:, :, 0:CONTEXTS], axis=mybir.AxisListType.X, op=ALU.add
-        )
+        weight_cols = keep.tile([P, NODE_TILES, P], BF16)
+        nc.gpsimd.memset(weight_cols[:].rearrange("p t c -> p (t c)").bitcast(F32), 0.0)
+        nc.vector.tensor_copy(out=weight_cols[:, :, 0 : CONTEXTS + 1], in_=weight[:])
+        weight_rows = keep.tile([P, NODE_TILES, P], BF16)
+        bias_sorted = keep.tile([P, HIDDEN], BF16)
 
-        bias_all = keep.tile([P, 2 * HIDDEN + OUTPUTS], F32)
-
-        def spread_biases(biases):
-            for cols in biases:
-                width = cols.stop - cols.start
-                spread = banks.tile([P, width], F32, tag="bank")
-                nc.tensor.matmul(out=spread[:], lhsT=ones[:], rhs=bias_rows[:, cols], start=True, stop=True)
-                if width == HIDDEN:
-                    nc.vector.tensor_copy(
-                        out=bias_all[:, cols].rearrange("p (c r) -> p c r", c=PACK),
-                        in_=spread[:].rearrange("p (r c) -> p c r", c=PACK),
-                    )
-                else:
-                    nc.vector.tensor_copy(out=bias_all[:, cols], in_=spread[:])
+        def prepare_biases():
+            turned = banks.tile([P, NODE_TILES, P], BF16, tag="bank")
+            for t in range(NODE_TILES):
+                nc.tensor.transpose(turned[:, t, :], weight_cols[:, t, :], identity_bf16[:])
+            nc.vector.tensor_copy(out=weight_rows[:], in_=turned[:])
+            nc.vector.tensor_copy(
+                out=bias_sorted[:].rearrange("p (c r) -> p c r", c=PACK),
+                in_=bias_rows[:].rearrange("p (r c) -> p c r", c=PACK),
+            )
 
         running = keep.tile([P, NODE_TILES, HIDDEN], F32)
 
         def start_running(t):
-            nc.vector.scalar_tensor_tensor(
-                out=running[:, t, :],
-                in0=bias_all[:, BC],
-                scalar=weight_sum[:, t : t + 1],
-                in1=bias_all[:, BN],
-                op0=ALU.mult,
-                op1=ALU.add,
-            )
+            biases = banks.tile([P, HIDDEN], F32, tag="bank")
+            nc.tensor.matmul(out=biases[:], lhsT=weight_rows[:, t, :], rhs=bias_sorted[:], start=True, stop=True)
+            nc.scalar.copy(out=running[:, t, :], in_=biases[:])
+
+        bu_all = keep.tile([P, OUTPUTS], F32)
+
+        def spread_bu():
+            spread = banks.tile([P, OUTPUTS], F32, tag="bank")
+            nc.tensor.matmul(out=spread[:], lhsT=ones[:], rhs=bu_row[:], start=True, stop=True)
+            nc.vector.tensor_copy(out=bu_all[:], in_=spread[:])
 
         def flip_block(i, grouped_words, copy=nc.scalar.copy):
             words = rows_of[i][:].bitcast(F32)
@@ -225,7 +226,7 @@ def tile_nodeembeddinglayer_pa_t_kernel(tc, x, contexts, attn, Wn, bn, Wc, bc, W
             )
 
         def flip_hidden(rows, grouped):
-            flipped = banks.tile([P, PACK, P], F32, tag="bank")
+            flipped = banks.tile([P, PACK, P], BF16, tag="bank")
             for c in range(PACK):
                 nc.tensor.matmul(
                     out=flipped[:, c, :], lhsT=rows[:, c * P : (c + 1) * P], rhs=identity_bf16[:], start=True, stop=True
@@ -266,11 +267,11 @@ def tile_nodeembeddinglayer_pa_t_kernel(tc, x, contexts, attn, Wn, bn, Wc, bc, W
             )
             result = tail_pool.tile([P, OUTPUTS], F32)
             if t == NODE_TILES - 1:
-                nc.vector.tensor_tensor(out=result[:], in0=projected[:], in1=bias_all[:, BU], op=ALU.add)
+                nc.vector.tensor_tensor(out=result[:], in0=projected[:], in1=bu_all[:], op=ALU.add)
             else:
                 unbiased = tail_pool.tile([P, OUTPUTS], F32)
                 nc.scalar.copy(out=unbiased[:], in_=projected[:])
-                nc.gpsimd.tensor_tensor(out=result[:], in0=unbiased[:], in1=bias_all[:, BU], op=ALU.add)
+                nc.gpsimd.tensor_tensor(out=result[:], in0=unbiased[:], in1=bu_all[:], op=ALU.add)
             nc.sync.dma_start(out=out_tiles[t], in_=result[:])
 
         def blocks_of(q):
@@ -296,6 +297,8 @@ def tile_nodeembeddinglayer_pa_t_kernel(tc, x, contexts, attn, Wn, bn, Wc, bc, W
                 flip_output_weights(wu_grouped)
             if coming_rows:
                 grouped_pairs = flip_round(q + 1)
+            if q == FIRST_ROWS:
+                start_running(0)
             to_sort = q + 1 + SORT_AHEAD
             if FIRST_SORTED <= to_sort < len(rounds):
                 for j in range(BLOCKS):
@@ -312,9 +315,6 @@ def tile_nodeembeddinglayer_pa_t_kernel(tc, x, contexts, attn, Wn, bn, Wc, bc, W
             for j in range(BLOCKS):
                 if coming_rows and j in QUANTISE_BEFORE:
                     following.append(quantise_pair(grouped_pairs[len(following)]))
-                    if q + 1 == FIRST_ROWS and len(following) == 1:
-                        spread_biases((BC, BN))
-                        start_running(0)
                 if multiplied:
                     t, k = multiplied[j]
                     sums = multiply_block(operands, j, weights_of[WN if k == ONE else WC])
@@ -331,9 +331,6 @@ def tile_nodeembeddinglayer_pa_t_kernel(tc, x, contexts, attn, Wn, bn, Wc, bc, W
                 if j == BLOCKS - 2:
                     for t in early:
                         hidden_operand = quantise_hidden(hidden_grouped, tail_pool, "hidden", P)
-            for t, k in coming_rows:
-                if k == 0 and t > 0:
-                    start_running(t)
             if coming_rows:
                 operands = following
             if coming == WC:
@@ -341,6 +338,11 @@ def tile_nodeembeddinglayer_pa_t_kernel(tc, x, contexts, attn, Wn, bn, Wc, bc, W
             if 0 <= q < len(rounds) and rounds[q] == WN:
                 weights_of[WN] = quantise_weights(weights_grouped, WN)
                 weights_of["wu"] = quantise_hidden(wu_grouped, keep, "wu", OUTPUTS)
-                spread_biases((BU,))
+                spread_bu()
             for t in done + early:
                 project(hidden_operand, weights_of["wu"], t)
+            if q + 1 == FIRST_ROWS:
+                prepare_biases()
+            for t, k in coming_rows:
+                if k == 0 and t > 0:
+                    start_running(t)

@@ -37,12 +37,15 @@ PAIR_BUFS = 3 * BLOCKS // PAIR
 def plan_rounds():
     first_half = [[(t, k) for k in range(HALF)] for t in range(NODE_TILES)]
     second_half = [[(t, k) for k in [HALF, HALF + 1, ONE] + list(range(HALF + 2, CONTEXTS))] for t in range(NODE_TILES)]
+
+    def spread_evenly(a, b):
+        places = [((i + 0.5) / len(part), block) for part in (a, b) for i, block in enumerate(part)]
+        return [block for place, block in sorted(places)]
+
     blocks = list(first_half[0])
-    for t in range(NODE_TILES - 1):
-        for i in range(len(second_half[t])):
-            blocks.append(second_half[t][i])
-            blocks.extend(first_half[t + 1][i : i + 1])
-    blocks.extend(second_half[NODE_TILES - 1])
+    for t in range(NODE_TILES - 2):
+        blocks.extend(spread_evenly(second_half[t], first_half[t + 1]))
+    blocks.extend(spread_evenly(second_half[-2], first_half[-1] + second_half[-1]))
     row_rounds = [blocks[i : i + BLOCKS] for i in range(0, len(blocks), BLOCKS)]
     return [WC, row_rounds[0], WN] + row_rounds[1:]
 
@@ -87,7 +90,10 @@ def tile_nodeembeddinglayer_pa_t_kernel(tc, x, contexts, attn, Wn, bn, Wc, bc, W
 
         def load_block(i):
             raw = raw_pool.tile([P, FEATURES], BF16)
-            nc.sync.dma_start(out=raw[:], in_=sources[i])
+            pieces = PASSES if i == 0 else 1
+            for c in range(pieces):
+                cols = slice(c * FEATURES // pieces, (c + 1) * FEATURES // pieces)
+                nc.sync.dma_start(out=raw[:, cols], in_=sources[i][:, cols])
             rows_of[i] = raw
 
         before_biases, before_wu = rounds.index(WN) * BLOCKS, (rounds.index(WN) + 1) * BLOCKS
@@ -284,11 +290,12 @@ def tile_nodeembeddinglayer_pa_t_kernel(tc, x, contexts, attn, Wn, bn, Wc, bc, W
             coming = rounds[q + 1] if q + 1 < len(rounds) else None
             coming_rows = blocks_of(q + 1)
 
-            done = [t for t, k in blocks_of(q - 2) if k == CONTEXTS - 1 and q != len(rounds)]
-            early = [t for t, k in blocks_of(q - 1) if k == CONTEXTS - 1 and q == len(rounds) - 1]
+            done = [t for t, k in blocks_of(q - 2) if k == CONTEXTS - 1]
+            hidden_grouped = {}
             for t in done:
-                hidden_grouped = tail_pool.tile([P, P, PACK], BF16, align_bytes=64)
-                flip_hidden(hidden_of[t][:], hidden_grouped[:])
+                grouped = tail_pool.tile([P, P, PACK], BF16, align_bytes=64)
+                flip_hidden(hidden_of[t][:], grouped[:])
+                hidden_grouped[t] = grouped
             if coming == WC:
                 weights_grouped = flip_weights(q + 1, coming, (nc.scalar.copy, nc.vector.tensor_copy))
             if coming == WN:
@@ -308,8 +315,9 @@ def tile_nodeembeddinglayer_pa_t_kernel(tc, x, contexts, attn, Wn, bn, Wc, bc, W
                 for j in range(BLOCKS):
                     sort_words((FIRST_SORTED - 1) * BLOCKS + j, nc.vector.tensor_copy)
 
+            hidden_operands = {}
             for t in done:
-                hidden_operand = quantise_hidden(hidden_grouped, tail_pool, "hidden", P)
+                hidden_operands[t] = quantise_hidden(hidden_grouped[t], tail_pool, "hidden", P)
             following = []
             multiplied = blocks_of(q)
             for j in range(BLOCKS):
@@ -324,13 +332,6 @@ def tile_nodeembeddinglayer_pa_t_kernel(tc, x, contexts, attn, Wn, bn, Wc, bc, W
                         hidden_of[t] = hidden
                     else:
                         add_weighted(sums, t, k, running[:, t, :])
-                if j == PAIR - 1:
-                    for t in early:
-                        hidden_grouped = tail_pool.tile([P, P, PACK], BF16, align_bytes=64)
-                        flip_hidden(hidden_of[t][:], hidden_grouped[:])
-                if j == BLOCKS - 2:
-                    for t in early:
-                        hidden_operand = quantise_hidden(hidden_grouped, tail_pool, "hidden", P)
             if coming_rows:
                 operands = following
             if coming == WC:
@@ -339,8 +340,8 @@ def tile_nodeembeddinglayer_pa_t_kernel(tc, x, contexts, attn, Wn, bn, Wc, bc, W
                 weights_of[WN] = quantise_weights(weights_grouped, WN)
                 weights_of["wu"] = quantise_hidden(wu_grouped, keep, "wu", OUTPUTS)
                 spread_bu()
-            for t in done + early:
-                project(hidden_operand, weights_of["wu"], t)
+            for t in done:
+                project(hidden_operands[t], weights_of["wu"], t)
             if q + 1 == FIRST_ROWS:
                 prepare_biases()
             for t, k in coming_rows:

from contextlib import ExitStack

import concourse.mybir as mybir
from concourse.masks import make_identity

F32 = mybir.dt.float32
BF16 = mybir.dt.bfloat16
U32 = mybir.dt.uint32
U8 = mybir.dt.uint8
FP8X4 = mybir.dt.float8_e4m3fn_x4
ALU = mybir.AluOpType

P = 128
PACK = 4
K_PASS = P * PACK

NODES, CONTEXTS, FEATURES, HIDDEN, OUTPUTS = 1024, 8, 1024, 512, 256
NODE_TILES = NODES // P
PASSES = FEATURES // K_PASS
WORD_PIECES = FEATURES // 2 // P

BLOCKS = 4
HALF = CONTEXTS // 2
ONE = CONTEXTS
WN, WC = "wn", "wc"

PAIR = 2
RAW_BUFS = 12 * BLOCKS
SORT_AHEAD = 2
SORTERS = ("scalar", "scalar", "gpsimd", "gpsimd")
FIRST_ROWS = 1
FIRST_SORTED = 4
QUANTISE_BEFORE = (1, 2)
PAIR_BUFS = 3 * BLOCKS // PAIR


def plan_rounds():
    first_half = [[(t, k) for k in range(HALF)] for t in range(NODE_TILES)]
    second_half = [[(t, k) for k in [HALF, HALF + 1, ONE] + list(range(HALF + 2, CONTEXTS))] for t in range(NODE_TILES)]

    def spread_evenly(a, b):
        places = [((i + 0.5) / len(part), block) for part in (a, b) for i, block in enumerate(part)]
        return [block for place, block in sorted(places)]

    blocks = list(first_half[0])
    for t in range(NODE_TILES - 2):
        blocks.extend(spread_evenly(second_half[t], first_half[t + 1]))
    blocks.extend(spread_evenly(second_half[-2], first_half[-1] + second_half[-1]))
    row_rounds = [blocks[i : i + BLOCKS] for i in range(0, len(blocks), BLOCKS)]
    return [WC, row_rounds[0], WN] + row_rounds[1:]


FLOPS = 2 * NODES * (CONTEXTS + 1) * FEATURES * HIDDEN + 2 * NODES * HIDDEN * OUTPUTS


def tile_nodeembeddinglayer_pa_t_kernel(tc, x, contexts, attn, Wn, bn, Wc, bc, Wu, bu, out):
    nc = tc.nc
    with ExitStack() as stack:
        keep = stack.enter_context(tc.tile_pool(name="keep", bufs=1))
        raw_pool = stack.enter_context(tc.tile_pool(name="raw_pool", bufs=RAW_BUFS))
        pair_pool = stack.enter_context(tc.tile_pool(name="pair_pool", bufs=PAIR_BUFS))
        sorted_pool = stack.enter_context(tc.tile_pool(name="sorted_pool", bufs=(SORT_AHEAD + 1) * BLOCKS))
        tail_pool = stack.enter_context(tc.tile_pool(name="tail_pool", bufs=2))
        banks = stack.enter_context(tc.psum_pool(name="banks", bufs=2 * BLOCKS))
        stack.enter_context(tc.manual_schedule())

        attn_sb = keep.tile([P, NODE_TILES, CONTEXTS], BF16)
        nc.scalar.dma_start(out=attn_sb[:], in_=attn.rearrange("(p t) k -> p t k", t=NODE_TILES))
        bias_rows = keep.tile([P, HIDDEN], BF16)
        bu_row = keep.tile([P, OUTPUTS], BF16)
        nc.vector.memset(bias_rows[:].bitcast(F32), 0.0)
        nc.vector.memset(bu_row[:].bitcast(F32), 0.0)

        x_blocks = x.rearrange("(p t) f -> t p f", t=NODE_TILES)
        context_blocks = contexts.rearrange("(p t) k f -> (t k) p f", t=NODE_TILES)
        wn_blocks = Wn.rearrange("(p c) f -> c p f", c=PACK)
        wc_blocks = Wc.rearrange("(p c) f -> c p f", c=PACK)
        rounds = plan_rounds()
        sources = []
        for blocks in rounds:
            if blocks == WN or blocks == WC:
                weight_blocks = wn_blocks if blocks == WN else wc_blocks
                sources.extend([weight_blocks[b] for b in range(BLOCKS)])
            else:
                sources.extend([x_blocks[t] if k == ONE else context_blocks[t * CONTEXTS + k] for t, k in blocks])
        out_tiles = out.rearrange("(p t) o -> t p o", t=NODE_TILES)

        rows_of = {}
        sorted_of = {}

        def load_block(i):
            raw = raw_pool.tile([P, FEATURES], BF16)
            pieces = PASSES if i == 0 else 1
            for c in range(pieces):
                cols = slice(c * FEATURES // pieces, (c + 1) * FEATURES // pieces)
                nc.sync.dma_start(out=raw[:, cols], in_=sources[i][:, cols])
            rows_of[i] = raw

        before_biases, before_wu = rounds.index(WN) * BLOCKS, (rounds.index(WN) + 1) * BLOCKS
        for i in range(before_biases):
            load_block(i)
        nc.sync.dma_start(out=bias_rows[0:CONTEXTS, :], in_=bc.partition_broadcast(CONTEXTS))
        nc.sync.dma_start(out=bias_rows[ONE : ONE + 1, :], in_=bn.unsqueeze(0))
        nc.sync.dma_start(out=bu_row[0:1, :], in_=bu.unsqueeze(0))
        for i in range(before_biases, before_wu):
            load_block(i)
        wu_raw = keep.tile([P, OUTPUTS // P, HIDDEN], BF16)
        nc.sync.dma_start(out=wu_raw[:], in_=Wu.rearrange("(b p) h -> p b h", p=P))
        for i in range(before_wu, RAW_BUFS):
            load_block(i)

        identity_f32 = keep.tile([P, P], F32)
        make_identity(nc, identity_f32[:])
        identity_bf16 = keep.tile([P, P], BF16)
        make_identity(nc, identity_bf16[:])
        ones = keep.tile([P, P], BF16)
        nc.vector.memset(ones[:], 1.0)

        weight = keep.tile([P, NODE_TILES, CONTEXTS + 1], F32)
        nc.vector.memset(weight[:], 1.0)
        nc.vector.tensor_scalar_mul(out=weight[:, :, 0:CONTEXTS], in0=attn_sb[:], scalar1=1.0 / CONTEXTS)
        weight_cols = keep.tile([P, NODE_TILES, P], BF16)
        nc.gpsimd.memset(weight_cols[:].rearrange("p t c -> p (t c)").bitcast(F32), 0.0)
        nc.vector.tensor_copy(out=weight_cols[:, :, 0 : CONTEXTS + 1], in_=weight[:])
        weight_rows = keep.tile([P, NODE_TILES, P], BF16)
        bias_sorted = keep.tile([P, HIDDEN], BF16)

        def prepare_biases():
            turned = banks.tile([P, NODE_TILES, P], BF16, tag="bank")
            for t in range(NODE_TILES):
                nc.tensor.transpose(turned[:, t, :], weight_cols[:, t, :], identity_bf16[:])
            nc.vector.tensor_copy(out=weight_rows[:], in_=turned[:])
            nc.vector.tensor_copy(
                out=bias_sorted[:].rearrange("p (c r) -> p c r", c=PACK),
                in_=bias_rows[:].rearrange("p (r c) -> p c r", c=PACK),
            )

        running = keep.tile([P, NODE_TILES, HIDDEN], F32)

        def start_running(t):
            biases = banks.tile([P, HIDDEN], F32, tag="bank")
            nc.tensor.matmul(out=biases[:], lhsT=weight_rows[:, t, :], rhs=bias_sorted[:], start=True, stop=True)
            nc.scalar.copy(out=running[:, t, :], in_=biases[:])

        bu_all = keep.tile([P, OUTPUTS], F32)

        def spread_bu():
            spread = banks.tile([P, OUTPUTS], F32, tag="bank")
            nc.tensor.matmul(out=spread[:], lhsT=ones[:], rhs=bu_row[:], start=True, stop=True)
            nc.vector.tensor_copy(out=bu_all[:], in_=spread[:])

        def flip_block(i, grouped_words, copy=nc.scalar.copy):
            words = rows_of[i][:].bitcast(F32)
            flipped = banks.tile([P, WORD_PIECES, P], F32, tag="bank")
            for g in range(PASSES):
                for u in range(2):
                    if i in sorted_of:
                        piece = sorted_of[i][:, 2 * g + u, :]
                    else:
                        piece = words[:, 2 * P * g + u : 2 * P * (g + 1) : 2]
                    nc.tensor.transpose(flipped[:, 2 * g + u, :], piece, identity_f32[:])
            copy(out=grouped_words, in_=flipped[:].rearrange("p (g u) r -> p g r u", u=2))
            if i + RAW_BUFS < len(sources):
                load_block(i + RAW_BUFS)

        sort_copy = {"scalar": nc.scalar.copy, "gpsimd": nc.gpsimd.tensor_copy, "vector": nc.vector.tensor_copy}

        def sort_words(i, copy):
            ordered = sorted_pool.tile([P, WORD_PIECES, P], F32)
            copy(
                out=ordered[:].rearrange("p (g u) m -> p g u m", u=2),
                in_=rows_of[i][:].bitcast(F32).rearrange("p (g m u) -> p g u m", g=PASSES, u=2),
            )
            sorted_of[i] = ordered

        def flip_round(q):
            pairs = []
            for first in range(0, BLOCKS, PAIR):
                grouped = pair_pool.tile([P, PAIR * PASSES * P * PACK], BF16, align_bytes=64)
                words = grouped[:].bitcast(F32).rearrange("p (j g r u) -> p j g r u", j=PAIR, g=PASSES, u=2)
                for j in range(PAIR):
                    flip_block(q * BLOCKS + first + j, words[:, j])
                pairs.append(grouped)
            return pairs

        def quantise_pair(grouped):
            codes = pair_pool.tile([P, PAIR * PASSES * P], U32, align_bytes=64)
            scales = pair_pool.tile([P, PAIR * PASSES * P], U8, align_bytes=64)
            nc.vector.quantize_mx(out=codes[:].bitcast(FP8X4), scales=scales[:], in_=grouped[:])
            return codes, scales

        def flip_weights(q, label, copies):
            grouped = keep.tile([P, PASSES * HIDDEN * PACK], BF16, align_bytes=64, name=label + "_grouped")
            by_block = grouped[:].bitcast(F32).rearrange("p (g b r u) -> p b g r u", g=PASSES, b=BLOCKS, u=2)
            for b in range(BLOCKS):
                flip_block(q * BLOCKS + b, by_block[:, b], copies[b % len(copies)])
            return grouped

        def quantise_weights(grouped, label):
            codes = keep.tile([P, PASSES * HIDDEN], U32, align_bytes=64, name=label + "_codes")
            scales = keep.tile([P, PASSES * HIDDEN], U8, align_bytes=64, name=label + "_scales")
            nc.vector.quantize_mx(out=codes[:].bitcast(FP8X4), scales=scales[:], in_=grouped[:])
            return codes, scales

        def multiply_block(pairs, j, weights):
            codes, scales = pairs[j // PAIR]
            w_codes, w_scales = weights
            sums = banks.tile([P, HIDDEN], F32, tag="bank")
            for g in range(PASSES):
                first = (j % PAIR * PASSES + g) * P
                rows = slice(first, first + P)
                hidden_cols = slice(g * HIDDEN, (g + 1) * HIDDEN)
                nc.tensor.matmul_mx(
                    out=sums[:],
                    lhsT=codes[:, rows].bitcast(FP8X4),
                    lhsT_scale=scales[:, rows],
                    rhs=w_codes[:, hidden_cols].bitcast(FP8X4),
                    rhs_scale=w_scales[:, hidden_cols],
                    start=(g == 0),
                    stop=(g == PASSES - 1),
                )
            return sums

        def add_weighted(sums, t, column, target):
            nc.vector.scalar_tensor_tensor(
                out=target,
                in0=sums[:],
                scalar=weight[:, t, column : column + 1],
                in1=running[:, t, :],
                op0=ALU.mult,
                op1=ALU.add,
            )

        def flip_hidden(rows, grouped):
            flipped = banks.tile([P, PACK, P], BF16, tag="bank")
            for c in range(PACK):
                nc.tensor.matmul(
                    out=flipped[:, c, :], lhsT=rows[:, c * P : (c + 1) * P], rhs=identity_bf16[:], start=True, stop=True
                )
            nc.scalar.copy(out=grouped, in_=flipped[:].rearrange("p c r -> p r c"))

        def flip_output_weights(grouped):
            flipped = banks.tile([P, OUTPUTS // P, 2, P], F32, tag="bank")
            for b in range(OUTPUTS // P):
                words = wu_raw[:, b, :].bitcast(F32)
                for u in range(2):
                    nc.tensor.transpose(flipped[:, b, u, :], words[:, u : HIDDEN // 2 : 2], identity_f32[:])
            nc.scalar.copy(
                out=grouped[:].rearrange("p o c -> p (o c)").bitcast(F32).rearrange("p (b o u) -> p b o u", u=2, o=P),
                in_=flipped[:].rearrange("p b u o -> p b o u"),
            )

        def quantise_hidden(grouped, pool, label, count):
            codes = pool.tile([P, count], U32, align_bytes=64, name=label + "_codes")
            scales = pool.tile([P, count], U8, align_bytes=64, name=label + "_scales")
            nc.vector.quantize_mx(
                out=codes[:].bitcast(FP8X4), scales=scales[:], in_=grouped[:].rearrange("p r c -> p (r c)")
            )
            return codes, scales

        def project(operand, weights, t):
            codes, scales = operand
            w_codes, w_scales = weights
            projected = banks.tile([P, OUTPUTS], F32, tag="bank")
            nc.tensor.matmul_mx(
                out=projected[:],
                lhsT=codes[:].bitcast(FP8X4),
                lhsT_scale=scales[:],
                rhs=w_codes[:].bitcast(FP8X4),
                rhs_scale=w_scales[:],
                start=True,
                stop=True,
            )
            result = tail_pool.tile([P, OUTPUTS], F32)
            if t == NODE_TILES - 1:
                nc.vector.tensor_tensor(out=result[:], in0=projected[:], in1=bu_all[:], op=ALU.add)
            else:
                unbiased = tail_pool.tile([P, OUTPUTS], F32)
                nc.scalar.copy(out=unbiased[:], in_=projected[:])
                nc.gpsimd.tensor_tensor(out=result[:], in0=unbiased[:], in1=bu_all[:], op=ALU.add)
            nc.sync.dma_start(out=out_tiles[t], in_=result[:])

        def blocks_of(q):
            return rounds[q] if 0 <= q < len(rounds) and rounds[q] != WN and rounds[q] != WC else []

        weights_of = {}
        hidden_of = {}
        operands = []
        for q in range(-1, len(rounds) + 2):
            coming = rounds[q + 1] if q + 1 < len(rounds) else None
            coming_rows = blocks_of(q + 1)

            done = [t for t, k in blocks_of(q - 2) if k == CONTEXTS - 1]
            hidden_grouped = {}
            for t in done:
                grouped = tail_pool.tile([P, P, PACK], BF16, align_bytes=64)
                flip_hidden(hidden_of[t][:], grouped[:])
                hidden_grouped[t] = grouped
            if coming == WC:
                weights_grouped = flip_weights(q + 1, coming, (nc.scalar.copy, nc.vector.tensor_copy))
            if coming == WN:
                weights_grouped = flip_weights(q + 1, coming, (nc.scalar.copy,))
                wu_grouped = keep.tile([P, OUTPUTS, PACK], BF16, align_bytes=64)
                flip_output_weights(wu_grouped)
            if coming_rows:
                grouped_pairs = flip_round(q + 1)
            if q == FIRST_ROWS:
                start_running(0)
            to_sort = q + 1 + SORT_AHEAD
            if FIRST_SORTED <= to_sort < len(rounds):
                for j in range(BLOCKS):
                    sort_words(to_sort * BLOCKS + j, sort_copy[SORTERS[j]])

            if q + 2 == FIRST_SORTED - 1:
                for j in range(BLOCKS):
                    sort_words((FIRST_SORTED - 1) * BLOCKS + j, nc.vector.tensor_copy)

            hidden_operands = {}
            for t in done:
                hidden_operands[t] = quantise_hidden(hidden_grouped[t], tail_pool, "hidden", P)
            following = []
            multiplied = blocks_of(q)
            for j in range(BLOCKS):
                if coming_rows and j in QUANTISE_BEFORE:
                    following.append(quantise_pair(grouped_pairs[len(following)]))
                if multiplied:
                    t, k = multiplied[j]
                    sums = multiply_block(operands, j, weights_of[WN if k == ONE else WC])
                    if k == CONTEXTS - 1:
                        hidden = tail_pool.tile([P, HIDDEN], BF16)
                        add_weighted(sums, t, k, hidden[:])
                        hidden_of[t] = hidden
                    else:
                        add_weighted(sums, t, k, running[:, t, :])
            if coming_rows:
                operands = following
            if coming == WC:
                weights_of[WC] = quantise_weights(weights_grouped, WC)
            if 0 <= q < len(rounds) and rounds[q] == WN:
                weights_of[WN] = quantise_weights(weights_grouped, WN)
                weights_of["wu"] = quantise_hidden(wu_grouped, keep, "wu", OUTPUTS)
                spread_bu()
            for t in done:
                project(hidden_operands[t], weights_of["wu"], t)
            if q + 1 == FIRST_ROWS:
                prepare_biases()
            for t, k in coming_rows:
                if k == 0 and t > 0:
                    start_running(t)
